import numpy as np
import ml_dtypes


def mxq(x, axis, fmt="e4m3"):
    dtype, down = {"e4m3": (ml_dtypes.float8_e4m3fn, 7), "e5m2": (ml_dtypes.float8_e5m2, 14)}[fmt]
    v = np.moveaxis(np.asarray(x, np.float32).astype(ml_dtypes.bfloat16).astype(np.float64), axis, -1)
    blocks = v.reshape(v.shape[:-1] + (-1, 32))
    amax = np.abs(blocks).max(-1, keepdims=True)
    byte = np.maximum(np.where(amax > 0, np.frexp(amax)[1] - 1 + 127, 0) - down, 1)
    scale = np.exp2(byte - 127.0)
    codes = (blocks / scale).astype(np.float32).astype(dtype).astype(np.float64)
    return np.moveaxis((codes * scale).reshape(v.shape), -1, axis)


WIDE = False


def mx_kscale(k):
    if not WIDE:
        return np.ones(k)
    levels = np.array([10, -10, 5, -5, 0])
    a = np.random.permutation(np.resize(levels, k // 512 * 4)).reshape(k // 512, 4)
    idx = np.arange(k)
    return np.exp2(a[idx // 512, idx % 128 // 32])


BF16 = ml_dtypes.bfloat16


def bf(x):
    return np.asarray(x, np.float32).astype(BF16)


def f64(x):
    return np.asarray(x).astype(np.float64)


B, S, D, QK, E, V, QB = 8, 1024, 1024, 64, 64, 32, 512
W = 2 * QK + 2 * E
EPS = 1e-5


def erf(z):
    a = np.minimum(np.abs(z), 6.0)
    a2 = 2.0 * a * a
    term = a.copy()
    total = a.copy()
    for n in range(1, 120):
        term = term * a2 / (2 * n + 1)
        total = total + term
    return np.sign(z) * (2.0 / np.sqrt(np.pi)) * np.exp(-a * a) * total


def gelu_erf(v):
    return 0.5 * v * (1.0 + erf(v / np.sqrt(2.0)))


def setup_inputs():
    s = mx_kscale(D)
    x = np.random.standard_normal((B, S, D)) * (0.5 + np.random.random((B, S, 1))) + 0.5 * np.random.standard_normal((B, S, 1))
    return {"x": bf(x),
            "expand": bf(np.random.standard_normal((W, D)) / np.sqrt(D) / s),
            "ln_gamma": bf((1.0 + 0.1 * np.random.standard_normal(D)) * s),
            "ln_beta": bf(0.1 * np.random.standard_normal(D) * s)}


def reference(x, expand, ln_gamma, ln_beta):
    x = f64(x)
    mu = x.mean(-1, keepdims=True)
    var = x.var(-1, keepdims=True)
    h = (x - mu) / np.sqrt(var + EPS) * f64(ln_gamma) + f64(ln_beta)
    proj = mxq(h, 2, "e4m3") @ mxq(f64(expand), 1, "e4m3").T
    q = proj[..., :QK]
    k = proj[..., QK:2 * QK]
    lin = proj[..., 2 * QK:2 * QK + E]
    pre_gelu = proj[..., 2 * QK + E:]
    geglu = lin * gelu_erf(pre_gelu)
    return q, k, geglu[..., :E - V], geglu[..., E - V:]

@@ -1,0 +1,184 @@
+from contextlib import ExitStack
+
+import concourse.mybir as mybir
+from concourse.masks import make_identity
+
+F32 = mybir.dt.float32
+BF16 = mybir.dt.bfloat16
+U32 = mybir.dt.uint32
+U8 = mybir.dt.uint8
+FP8X4 = mybir.dt.float8_e4m3fn_x4
+ALU = mybir.AluOpType
+ACT = mybir.ActivationFunctionType
+
+P = 128
+PACK = 4
+ROWS = 8 * 1024
+D = 1024
+CHUNKS = D // P
+PASSES = CHUNKS // PACK
+J = 4
+GROUP = J * P
+GROUPS = ROWS // GROUP
+QK = 64
+E = 64
+V = 32
+W = 2 * QK + 2 * E
+EPS = 1e-5
+BN_MAX = 512
+
+FLOPS = 2 * ROWS * D * W
+
+
+def tile_latentattentionblock_pa_t_kernel(tc, x, expand, ln_gamma, ln_beta, out_0, out_1, out_2, out_3):
+    nc = tc.nc
+    x_rows = x.flatten_outer_dims()
+    outs = [o.flatten_outer_dims() for o in (out_0, out_1, out_2, out_3)]
+
+    with ExitStack() as stack:
+        const = stack.enter_context(tc.tile_pool(name="const", bufs=1))
+        x_pool = stack.enter_context(tc.tile_pool(name="x", bufs=4))
+        small = stack.enter_context(tc.tile_pool(name="small", bufs=4))
+        z_pool = stack.enter_context(tc.tile_pool(name="z", bufs=2))
+        h_pool = stack.enter_context(tc.tile_pool(name="h", bufs=2))
+        mx_pool = stack.enter_context(tc.tile_pool(name="mx", bufs=2))
+        out_pool = stack.enter_context(tc.tile_pool(name="out", bufs=3))
+        turn = stack.enter_context(tc.psum_pool(name="turn", bufs=6))
+        acc = stack.enter_context(tc.psum_pool(name="acc", bufs=1))
+
+        ident_f32 = const.tile([P, P], F32)
+        make_identity(nc, ident_f32[:])
+        ident_bf16 = const.tile([P, P], BF16)
+        make_identity(nc, ident_bf16[:])
+        minus_half = const.tile([P, J], F32)
+        nc.vector.memset(minus_half[:], -0.5)
+
+        vec_rows = const.tile([P, P], BF16)
+        nc.vector.memset(vec_rows[:], 0.0)
+        nc.scalar.dma_start(out=vec_rows[0:CHUNKS, :], in_=ln_gamma.rearrange("(c p) -> c p", p=P))
+        nc.scalar.dma_start(out=vec_rows[CHUNKS : 2 * CHUNKS, :], in_=ln_beta.rearrange("(c p) -> c p", p=P))
+        vec_cols = turn.tile([P, P], BF16, tag="bank")
+        nc.tensor.transpose(vec_cols[:], vec_rows[:], ident_bf16[:])
+        gain_shift = const.tile([P, 2 * CHUNKS], F32)
+        nc.vector.tensor_copy(out=gain_shift[:], in_=vec_cols[:, 0 : 2 * CHUNKS])
+
+        e_sb = const.tile([P, W // P, D], BF16)
+        nc.scalar.dma_start(out=e_sb[:], in_=expand.rearrange("(h f) k -> f h k", f=P))
+        e_grouped = const.tile([P, PASSES, W, PACK], BF16, align_bytes=64)
+        for g in range(PASSES):
+            for half in range(W // P):
+                e_turned = turn.tile([P, PACK, P], BF16, tag="bank")
+                for t in range(PACK):
+                    c = PACK * g + t
+                    nc.tensor.transpose(e_turned[:, t, :], e_sb[:, half, c * P : (c + 1) * P], ident_bf16[:])
+                nc.vector.tensor_copy(
+                    out=e_grouped[:, g, half * P : (half + 1) * P, :],
+                    in_=e_turned[:].rearrange("p t f -> p f t"),
+                )
+        e_codes = const.tile([P, PASSES, W], U32, align_bytes=64)
+        e_scales = const.tile([P, PASSES, W], U8, align_bytes=64)
+        nc.vector.quantize_mx(
+            out=e_codes[:].rearrange("p g f -> p (g f)").bitcast(FP8X4),
+            scales=e_scales[:].rearrange("p g f -> p (g f)"),
+            in_=e_grouped[:].rearrange("p g f t -> p (g f t)"),
+        )
+
+        for s in range(GROUPS):
+            rows = slice(s * GROUP, (s + 1) * GROUP)
+
+            x_sb = x_pool.tile([P, J, D], BF16)
+            nc.sync.dma_start(out=x_sb[:], in_=x_rows[rows, :].rearrange("(p j) k -> p j k", j=J))
+
+            stats = small.tile([P, J, D // BN_MAX, 6], F32)
+            mean_var = small.tile([P, J, 2], F32)
+            for j in range(J):
+                for b in range(D // BN_MAX):
+                    nc.vector.bn_stats(out=stats[:, j, b, :], in_=x_sb[:, j, b * BN_MAX : (b + 1) * BN_MAX])
+                nc.vector.bn_aggr(out=mean_var[:, j, :], in_=stats[:, j, :, :].rearrange("p b s -> p (b s)"))
+            var_eps = small.tile([P, J], F32)
+            nc.gpsimd.tensor_scalar(out=var_eps[:], in0=mean_var[:, :, 1], scalar1=EPS, scalar2=None, op0=ALU.add)
+            rstd = small.tile([P, J], F32)
+            nc.gpsimd.tensor_tensor(out=rstd[:], in0=var_eps[:], in1=minus_half[:], op=ALU.pow)
+
+            minus_mean_rstd = small.tile([P, J], F32)
+            nc.vector.scalar_tensor_tensor(
+                out=minus_mean_rstd[:], in0=mean_var[:, :, 0], scalar=-1.0, in1=rstd[:], op0=ALU.mult, op1=ALU.mult
+            )
+
+            z = z_pool.tile([P, J, D], F32)
+            for j in range(J):
+                nc.gpsimd.tensor_scalar(
+                    out=z[:, j, :],
+                    in0=x_sb[:, j, :],
+                    scalar1=rstd[:, j : j + 1],
+                    scalar2=minus_mean_rstd[:, j : j + 1],
+                    op0=ALU.mult,
+                    op1=ALU.add,
+                )
+
+            h_turned = h_pool.tile([P, CHUNKS, GROUP], BF16)
+            for c in range(CHUNKS):
+                z_turned = turn.tile([P, J, P], F32, tag="bank")
+                for j in range(J):
+                    nc.tensor.transpose(z_turned[:, j, :], z[:, j, c * P : (c + 1) * P], ident_f32[:])
+                nc.scalar.activation(
+                    out=h_turned[:, c, :],
+                    in_=z_turned[:].rearrange("p j r -> p (j r)"),
+                    func=ACT.Identity,
+                    bias=gain_shift[:, CHUNKS + c : CHUNKS + c + 1],
+                    scale=gain_shift[:, c : c + 1],
+                )
+
+            h_grouped = h_pool.tile([P, PASSES, GROUP, PACK], BF16, align_bytes=64)
+            h_codes = mx_pool.tile([P, PASSES, GROUP], U32, align_bytes=64)
+            h_scales = mx_pool.tile([P, PASSES, GROUP], U8, align_bytes=64)
+            for g in range(PASSES):
+                nc.vector.tensor_copy(
+                    out=h_grouped[:, g, :, :].rearrange("p (r i) t -> p r t i", i=4),
+                    in_=h_turned[:, PACK * g : PACK * (g + 1), :].rearrange("p t (r i) -> p r t i", i=4),
+                )
+            for g in range(PASSES):
+                nc.vector.quantize_mx(
+                    out=h_codes[:, g, :].bitcast(FP8X4),
+                    scales=h_scales[:, g, :],
+                    in_=h_grouped[:, g, :, :].rearrange("p r t -> p (r t)"),
+                )
+
+            proj_qk = acc.tile([P, J, 2 * QK], F32)
+            proj_gate = acc.tile([P, J, 2 * E], F32)
+            for j in range(J):
+                for bank, first in ((proj_qk, 0), (proj_gate, 2 * QK)):
+                    for g in range(PASSES):
+                        nc.tensor.matmul_mx(
+                            out=bank[:, j, :],
+                            lhsT=h_codes[:, g, j * P : (j + 1) * P].bitcast(FP8X4),
+                            lhsT_scale=h_scales[:, g, j * P : (j + 1) * P],
+                            rhs=e_codes[:, g, first : first + P].bitcast(FP8X4),
+                            rhs_scale=e_scales[:, g, first : first + P],
+                            start=(g == 0),
+                            stop=(g == PASSES - 1),
+                        )
+
+            qk_sb = out_pool.tile([P, 2, J, QK], F32)
+            nc.scalar.copy(
+                out=qk_sb[:].rearrange("p w j c -> p j w c"),
+                in_=proj_qk[:].rearrange("p j (w c) -> p j w c", w=2),
+            )
+            gelu_sb = out_pool.tile([P, J, E], F32)
+            nc.scalar.activation(out=gelu_sb[:], in_=proj_gate[:, :, E : 2 * E], func=ACT.Gelu)
+            geglu_sb = out_pool.tile([P, 2, J, V], F32)
+            nc.vector.tensor_tensor(
+                out=geglu_sb[:].rearrange("p v j c -> p j v c"),
+                in0=proj_gate[:, :, 0:E].rearrange("p j (v c) -> p j v c", v=2),
+                in1=gelu_sb[:].rearrange("p j (v c) -> p j v c", v=2),
+                op=ALU.mult,
+            )
+            for plane in range(2):
+                nc.sync.dma_start(
+                    out=outs[plane][rows, :].rearrange("(p j) c -> p (j c)", j=J),
+                    in_=qk_sb[:, plane, :, :].rearrange("p j c -> p (j c)"),
+                )
+                nc.sync.dma_start(
+                    out=outs[2 + plane][rows, :].rearrange("(p j) c -> p (j c)", j=J),
+                    in_=geglu_sb[:, plane, :, :].rearrange("p j c -> p (j c)"),
+                )

@@ -27,6 +27,9 @@ W = 2 * QK + 2 * E
 EPS = 1e-5
 BN_MAX = 512
 
+J_VECTOR = 3
+LOADS_AHEAD = 3
+
 FLOPS = 2 * ROWS * D * W
 
 
@@ -38,13 +41,153 @@ def tile_latentattentionblock_pa_t_kernel(tc, x, expand, ln_gamma, ln_beta, out_
     with ExitStack() as stack:
         const = stack.enter_context(tc.tile_pool(name="const", bufs=1))
         x_pool = stack.enter_context(tc.tile_pool(name="x", bufs=4))
-        small = stack.enter_context(tc.tile_pool(name="small", bufs=4))
+        small = stack.enter_context(tc.tile_pool(name="small", bufs=3))
         z_pool = stack.enter_context(tc.tile_pool(name="z", bufs=2))
         h_pool = stack.enter_context(tc.tile_pool(name="h", bufs=2))
         mx_pool = stack.enter_context(tc.tile_pool(name="mx", bufs=2))
         out_pool = stack.enter_context(tc.tile_pool(name="out", bufs=3))
         turn = stack.enter_context(tc.psum_pool(name="turn", bufs=6))
         acc = stack.enter_context(tc.psum_pool(name="acc", bufs=1))
+
+        live = {}
+
+        def load(s):
+            x_sb = x_pool.tile([P, J, D], BF16)
+            nc.sync.dma_start(
+                out=x_sb[:], in_=x_rows[s * GROUP : (s + 1) * GROUP, :].rearrange("(p j) k -> p j k", j=J)
+            )
+            live["x", s] = x_sb
+
+        def statistics(s):
+            x_sb = live["x", s]
+            stats = small.tile([P, J, D // BN_MAX, 6], F32)
+            mean_var = small.tile([P, J, 2], F32)
+            for j in range(J):
+                for b in range(D // BN_MAX):
+                    nc.vector.bn_stats(out=stats[:, j, b, :], in_=x_sb[:, j, b * BN_MAX : (b + 1) * BN_MAX])
+                nc.vector.bn_aggr(out=mean_var[:, j, :], in_=stats[:, j, :, :].rearrange("p b s -> p (b s)"))
+            var_eps = small.tile([P, J], F32)
+            nc.gpsimd.tensor_scalar(out=var_eps[:], in0=mean_var[:, :, 1], scalar1=EPS, scalar2=None, op0=ALU.add)
+            rstd = small.tile([P, J], F32)
+            nc.gpsimd.tensor_tensor(out=rstd[:], in0=var_eps[:], in1=minus_half[:], op=ALU.pow)
+            live["mean_var", s] = mean_var
+            live["rstd", s] = rstd
+
+        def normalise(s):
+            x_sb, mean_var, rstd = live["x", s], live["mean_var", s], live["rstd", s]
+            minus_mean_rstd = small.tile([P, J], F32)
+            nc.vector.scalar_tensor_tensor(
+                out=minus_mean_rstd[:], in0=mean_var[:, :, 0], scalar=-1.0, in1=rstd[:], op0=ALU.mult, op1=ALU.mult
+            )
+            z = z_pool.tile([P, J, D], F32)
+            for j in range(J):
+                if j < J_VECTOR:
+                    nc.vector.tensor_scalar(
+                        out=z[:, j, :],
+                        in0=x_sb[:, j, :],
+                        scalar1=rstd[:, j : j + 1],
+                        scalar2=minus_mean_rstd[:, j : j + 1],
+                        op0=ALU.mult,
+                        op1=ALU.add,
+                    )
+                else:
+                    nc.scalar.activation(
+                        out=z[:, j, :],
+                        in_=x_sb[:, j, :],
+                        func=ACT.Identity,
+                        bias=minus_mean_rstd[:, j : j + 1],
+                        scale=rstd[:, j : j + 1],
+                    )
+            live["z", s] = z
+
+        def turn_and_scale(s):
+            z = live["z", s]
+            h_turned = h_pool.tile([P, CHUNKS, GROUP], BF16)
+            for c in range(CHUNKS):
+                z_turned = turn.tile([P, J, P], F32, tag="bank")
+                for j in range(J):
+                    nc.tensor.transpose(z_turned[:, j, :], z[:, j, c * P : (c + 1) * P], ident_f32[:])
+                nc.scalar.activation(
+                    out=h_turned[:, c, :],
+                    in_=z_turned[:].rearrange("p j r -> p (j r)"),
+                    func=ACT.Identity,
+                    bias=gain_shift[:, CHUNKS + c : CHUNKS + c + 1],
+                    scale=gain_shift[:, c : c + 1],
+                )
+            live["h_turned", s] = h_turned
+
+        def regroup(s):
+            h_turned = live["h_turned", s]
+            h_grouped = h_pool.tile([P, PASSES, GROUP, PACK], BF16, align_bytes=64)
+            for g, copy in ((0, nc.vector.tensor_copy), (1, nc.scalar.copy)):
+                copy(
+                    out=h_grouped[:, g, :, :].rearrange("p (r i) t -> p r t i", i=4),
+                    in_=h_turned[:, PACK * g : PACK * (g + 1), :].rearrange("p t (r i) -> p r t i", i=4),
+                )
+            live["h_grouped", s] = h_grouped
+            live["h_codes", s] = mx_pool.tile([P, PASSES, GROUP], U32, align_bytes=64, name="h_codes")
+            live["h_scales", s] = mx_pool.tile([P, PASSES, GROUP], U8, align_bytes=64, name="h_scales")
+
+        def quantise(s, g):
+            nc.vector.quantize_mx(
+                out=live["h_codes", s][:, g, :].bitcast(FP8X4),
+                scales=live["h_scales", s][:, g, :],
+                in_=live["h_grouped", s][:, g, :, :].rearrange("p r t -> p (r t)"),
+            )
+
+        def project(s):
+            h_codes, h_scales = live["h_codes", s], live["h_scales", s]
+            proj_qk = acc.tile([P, J, 2 * QK], F32)
+            proj_gate = acc.tile([P, J, 2 * E], F32)
+            for j in range(J):
+                for bank, first in ((proj_qk, 0), (proj_gate, 2 * QK)):
+                    for g in range(PASSES):
+                        nc.tensor.matmul_mx(
+                            out=bank[:, j, :],
+                            lhsT=h_codes[:, g, j * P : (j + 1) * P].bitcast(FP8X4),
+                            lhsT_scale=h_scales[:, g, j * P : (j + 1) * P],
+                            rhs=e_codes[:, g, first : first + P].bitcast(FP8X4),
+                            rhs_scale=e_scales[:, g, first : first + P],
+                            start=(g == 0),
+                            stop=(g == PASSES - 1),
+                        )
+            live["proj_qk", s] = proj_qk
+            live["proj_gate", s] = proj_gate
+
+        def leave_psum(s):
+            proj_qk = live["proj_qk", s]
+            qk_sb = out_pool.tile([P, 2, J, QK], F32)
+            nc.scalar.copy(
+                out=qk_sb[:].rearrange("p w j c -> p j w c"),
+                in_=proj_qk[:].rearrange("p j (w c) -> p j w c", w=2),
+            )
+            gelu_sb = out_pool.tile([P, J, E], F32)
+            nc.scalar.activation(out=gelu_sb[:], in_=live["proj_gate", s][:, :, E : 2 * E], func=ACT.Gelu)
+            live["qk_sb", s] = qk_sb
+            live["gelu_sb", s] = gelu_sb
+
+        def gate_and_store(s):
+            proj_gate, gelu_sb, qk_sb = live["proj_gate", s], live["gelu_sb", s], live["qk_sb", s]
+            geglu_sb = out_pool.tile([P, 2, J, V], F32)
+            nc.vector.tensor_tensor(
+                out=geglu_sb[:].rearrange("p v j c -> p j v c"),
+                in0=proj_gate[:, :, 0:E].rearrange("p j (v c) -> p j v c", v=2),
+                in1=gelu_sb[:].rearrange("p j (v c) -> p j v c", v=2),
+                op=ALU.mult,
+            )
+            rows = slice(s * GROUP, (s + 1) * GROUP)
+            for plane in range(2):
+                nc.sync.dma_start(
+                    out=outs[plane][rows, :].rearrange("(p j) c -> p (j c)", j=J),
+                    in_=qk_sb[:, plane, :, :].rearrange("p j c -> p (j c)"),
+                )
+                nc.sync.dma_start(
+                    out=outs[2 + plane][rows, :].rearrange("(p j) c -> p (j c)", j=J),
+                    in_=geglu_sb[:, plane, :, :].rearrange("p j c -> p (j c)"),
+                )
+
+        for s in range(LOADS_AHEAD):
+            load(s)
 
         ident_f32 = const.tile([P, P], F32)
         make_identity(nc, ident_f32[:])
@@ -83,102 +226,22 @@ def tile_latentattentionblock_pa_t_kernel(tc, x, expand, ln_gamma, ln_beta, out_
             in_=e_grouped[:].rearrange("p g f t -> p (g f t)"),
         )
 
-        for s in range(GROUPS):
-            rows = slice(s * GROUP, (s + 1) * GROUP)
-
-            x_sb = x_pool.tile([P, J, D], BF16)
-            nc.sync.dma_start(out=x_sb[:], in_=x_rows[rows, :].rearrange("(p j) k -> p j k", j=J))
-
-            stats = small.tile([P, J, D // BN_MAX, 6], F32)
-            mean_var = small.tile([P, J, 2], F32)
-            for j in range(J):
-                for b in range(D // BN_MAX):
-                    nc.vector.bn_stats(out=stats[:, j, b, :], in_=x_sb[:, j, b * BN_MAX : (b + 1) * BN_MAX])
-                nc.vector.bn_aggr(out=mean_var[:, j, :], in_=stats[:, j, :, :].rearrange("p b s -> p (b s)"))
-            var_eps = small.tile([P, J], F32)
-            nc.gpsimd.tensor_scalar(out=var_eps[:], in0=mean_var[:, :, 1], scalar1=EPS, scalar2=None, op0=ALU.add)
-            rstd = small.tile([P, J], F32)
-            nc.gpsimd.tensor_tensor(out=rstd[:], in0=var_eps[:], in1=minus_half[:], op=ALU.pow)
-
-            minus_mean_rstd = small.tile([P, J], F32)
-            nc.vector.scalar_tensor_tensor(
-                out=minus_mean_rstd[:], in0=mean_var[:, :, 0], scalar=-1.0, in1=rstd[:], op0=ALU.mult, op1=ALU.mult
-            )
-
-            z = z_pool.tile([P, J, D], F32)
-            for j in range(J):
-                nc.gpsimd.tensor_scalar(
-                    out=z[:, j, :],
-                    in0=x_sb[:, j, :],
-                    scalar1=rstd[:, j : j + 1],
-                    scalar2=minus_mean_rstd[:, j : j + 1],
-                    op0=ALU.mult,
-                    op1=ALU.add,
-                )
-
-            h_turned = h_pool.tile([P, CHUNKS, GROUP], BF16)
-            for c in range(CHUNKS):
-                z_turned = turn.tile([P, J, P], F32, tag="bank")
-                for j in range(J):
-                    nc.tensor.transpose(z_turned[:, j, :], z[:, j, c * P : (c + 1) * P], ident_f32[:])
-                nc.scalar.activation(
-                    out=h_turned[:, c, :],
-                    in_=z_turned[:].rearrange("p j r -> p (j r)"),
-                    func=ACT.Identity,
-                    bias=gain_shift[:, CHUNKS + c : CHUNKS + c + 1],
-                    scale=gain_shift[:, c : c + 1],
-                )
-
-            h_grouped = h_pool.tile([P, PASSES, GROUP, PACK], BF16, align_bytes=64)
-            h_codes = mx_pool.tile([P, PASSES, GROUP], U32, align_bytes=64)
-            h_scales = mx_pool.tile([P, PASSES, GROUP], U8, align_bytes=64)
-            for g in range(PASSES):
-                nc.vector.tensor_copy(
-                    out=h_grouped[:, g, :, :].rearrange("p (r i) t -> p r t i", i=4),
-                    in_=h_turned[:, PACK * g : PACK * (g + 1), :].rearrange("p t (r i) -> p r t i", i=4),
-                )
-            for g in range(PASSES):
-                nc.vector.quantize_mx(
-                    out=h_codes[:, g, :].bitcast(FP8X4),
-                    scales=h_scales[:, g, :],
-                    in_=h_grouped[:, g, :, :].rearrange("p r t -> p (r t)"),
-                )
-
-            proj_qk = acc.tile([P, J, 2 * QK], F32)
-            proj_gate = acc.tile([P, J, 2 * E], F32)
-            for j in range(J):
-                for bank, first in ((proj_qk, 0), (proj_gate, 2 * QK)):
-                    for g in range(PASSES):
-                        nc.tensor.matmul_mx(
-                            out=bank[:, j, :],
-                            lhsT=h_codes[:, g, j * P : (j + 1) * P].bitcast(FP8X4),
-                            lhsT_scale=h_scales[:, g, j * P : (j + 1) * P],
-                            rhs=e_codes[:, g, first : first + P].bitcast(FP8X4),
-                            rhs_scale=e_scales[:, g, first : first + P],
-                            start=(g == 0),
-                            stop=(g == PASSES - 1),
-                        )
-
-            qk_sb = out_pool.tile([P, 2, J, QK], F32)
-            nc.scalar.copy(
-                out=qk_sb[:].rearrange("p w j c -> p j w c"),
-                in_=proj_qk[:].rearrange("p j (w c) -> p j w c", w=2),
-            )
-            gelu_sb = out_pool.tile([P, J, E], F32)
-            nc.scalar.activation(out=gelu_sb[:], in_=proj_gate[:, :, E : 2 * E], func=ACT.Gelu)
-            geglu_sb = out_pool.tile([P, 2, J, V], F32)
-            nc.vector.tensor_tensor(
-                out=geglu_sb[:].rearrange("p v j c -> p j v c"),
-                in0=proj_gate[:, :, 0:E].rearrange("p j (v c) -> p j v c", v=2),
-                in1=gelu_sb[:].rearrange("p j (v c) -> p j v c", v=2),
-                op=ALU.mult,
-            )
-            for plane in range(2):
-                nc.sync.dma_start(
-                    out=outs[plane][rows, :].rearrange("(p j) c -> p (j c)", j=J),
-                    in_=qk_sb[:, plane, :, :].rearrange("p j c -> p (j c)"),
-                )
-                nc.sync.dma_start(
-                    out=outs[2 + plane][rows, :].rearrange("(p j) c -> p (j c)", j=J),
-                    in_=geglu_sb[:, plane, :, :].rearrange("p j c -> p (j c)"),
-                )
+        for i in range(-1, GROUPS + 2):
+            if i + 1 + LOADS_AHEAD < GROUPS:
+                load(i + 1 + LOADS_AHEAD)
+            if 0 <= i - 2:
+                project(i - 2)
+            if 0 <= i < GROUPS:
+                normalise(i)
+            if i + 1 < GROUPS:
+                statistics(i + 1)
+            if 0 <= i - 1 < GROUPS:
+                regroup(i - 1)
+            if 0 <= i - 2:
+                leave_psum(i - 2)
+                gate_and_store(i - 2)
+            if 0 <= i < GROUPS:
+                turn_and_scale(i)
+            if 0 <= i - 1 < GROUPS:
+                quantise(i - 1, 0)
+                quantise(i - 1, 1)

@@ -27,7 +27,7 @@ W = 2 * QK + 2 * E
 EPS = 1e-5
 BN_MAX = 512
 
-J_VECTOR = 3
+ROWS_VECTOR = 256
 LOADS_AHEAD = 3
 
 FLOPS = 2 * ROWS * D * W
@@ -58,14 +58,17 @@ def tile_latentattentionblock_pa_t_kernel(tc, x, expand, ln_gamma, ln_beta, out_
             )
             live["x", s] = x_sb
 
-        def statistics(s):
-            x_sb = live["x", s]
+        def partial_statistics(s):
             stats = small.tile([P, J, D // BN_MAX, 6], F32)
-            mean_var = small.tile([P, J, 2], F32)
             for j in range(J):
                 for b in range(D // BN_MAX):
-                    nc.vector.bn_stats(out=stats[:, j, b, :], in_=x_sb[:, j, b * BN_MAX : (b + 1) * BN_MAX])
-                nc.vector.bn_aggr(out=mean_var[:, j, :], in_=stats[:, j, :, :].rearrange("p b s -> p (b s)"))
+                    nc.vector.bn_stats(out=stats[:, j, b, :], in_=live["x", s][:, j, b * BN_MAX : (b + 1) * BN_MAX])
+            live["stats", s] = stats
+
+        def statistics(s):
+            mean_var = small.tile([P, J, 2], F32)
+            for j in range(J):
+                nc.vector.bn_aggr(out=mean_var[:, j, :], in_=live["stats", s][:, j, :, :].rearrange("p b s -> p (b s)"))
             var_eps = small.tile([P, J], F32)
             nc.gpsimd.tensor_scalar(out=var_eps[:], in0=mean_var[:, :, 1], scalar1=EPS, scalar2=None, op0=ALU.add)
             rstd = small.tile([P, J], F32)
@@ -73,32 +76,18 @@ def tile_latentattentionblock_pa_t_kernel(tc, x, expand, ln_gamma, ln_beta, out_
             live["mean_var", s] = mean_var
             live["rstd", s] = rstd
 
-        def normalise(s):
-            x_sb, mean_var, rstd = live["x", s], live["mean_var", s], live["rstd", s]
-            minus_mean_rstd = small.tile([P, J], F32)
-            nc.vector.scalar_tensor_tensor(
-                out=minus_mean_rstd[:], in0=mean_var[:, :, 0], scalar=-1.0, in1=rstd[:], op0=ALU.mult, op1=ALU.mult
-            )
-            z = z_pool.tile([P, J, D], F32)
-            for j in range(J):
-                if j < J_VECTOR:
-                    nc.vector.tensor_scalar(
-                        out=z[:, j, :],
-                        in0=x_sb[:, j, :],
-                        scalar1=rstd[:, j : j + 1],
-                        scalar2=minus_mean_rstd[:, j : j + 1],
-                        op0=ALU.mult,
-                        op1=ALU.add,
-                    )
-                else:
-                    nc.scalar.activation(
-                        out=z[:, j, :],
-                        in_=x_sb[:, j, :],
-                        func=ACT.Identity,
-                        bias=minus_mean_rstd[:, j : j + 1],
-                        scale=rstd[:, j : j + 1],
-                    )
-            live["z", s] = z
+        def normalise(s, row_tiles):
+            if ("z", s) not in live:
+                live["z", s] = z_pool.tile([P, J, D], F32, name="z")
+            for j in row_tiles:
+                nc.vector.tensor_scalar(
+                    out=live["z", s][:, j, :],
+                    in0=live["x", s][:, j, :],
+                    scalar1=live["mean_var", s][:, j, 0:1],
+                    scalar2=live["rstd", s][:, j : j + 1],
+                    op0=ALU.subtract,
+                    op1=ALU.mult,
+                )
 
         def turn_and_scale(s):
             z = live["z", s]
@@ -119,10 +108,14 @@ def tile_latentattentionblock_pa_t_kernel(tc, x, expand, ln_gamma, ln_beta, out_
         def regroup(s):
             h_turned = live["h_turned", s]
             h_grouped = h_pool.tile([P, PASSES, GROUP, PACK], BF16, align_bytes=64)
-            for g, copy in ((0, nc.vector.tensor_copy), (1, nc.scalar.copy)):
+            for copy, g, first, last in (
+                (nc.vector.tensor_copy, 0, 0, ROWS_VECTOR),
+                (nc.scalar.copy, 0, ROWS_VECTOR, GROUP),
+                (nc.scalar.copy, 1, 0, GROUP),
+            ):
                 copy(
-                    out=h_grouped[:, g, :, :].rearrange("p (r i) t -> p r t i", i=4),
-                    in_=h_turned[:, PACK * g : PACK * (g + 1), :].rearrange("p t (r i) -> p r t i", i=4),
+                    out=h_grouped[:, g, first:last, :].rearrange("p (r i) t -> p r t i", i=4),
+                    in_=h_turned[:, PACK * g : PACK * (g + 1), first:last].rearrange("p t (r i) -> p r t i", i=4),
                 )
             live["h_grouped", s] = h_grouped
             live["h_codes", s] = mx_pool.tile([P, PASSES, GROUP], U32, align_bytes=64, name="h_codes")
@@ -226,22 +219,28 @@ def tile_latentattentionblock_pa_t_kernel(tc, x, expand, ln_gamma, ln_beta, out_
             in_=e_grouped[:].rearrange("p g f t -> p (g f t)"),
         )
 
-        for i in range(-1, GROUPS + 2):
-            if i + 1 + LOADS_AHEAD < GROUPS:
-                load(i + 1 + LOADS_AHEAD)
-            if 0 <= i - 2:
-                project(i - 2)
-            if 0 <= i < GROUPS:
-                normalise(i)
-            if i + 1 < GROUPS:
-                statistics(i + 1)
-            if 0 <= i - 1 < GROUPS:
-                regroup(i - 1)
-            if 0 <= i - 2:
-                leave_psum(i - 2)
-                gate_and_store(i - 2)
-            if 0 <= i < GROUPS:
-                turn_and_scale(i)
-            if 0 <= i - 1 < GROUPS:
-                quantise(i - 1, 0)
-                quantise(i - 1, 1)
+        with tc.manual_schedule():
+            for i in range(-1, GROUPS + 2):
+                if i + 1 + LOADS_AHEAD < GROUPS:
+                    load(i + 1 + LOADS_AHEAD)
+                if i + 1 < GROUPS:
+                    partial_statistics(i + 1)
+                if 0 <= i - 2:
+                    project(i - 2)
+                if 0 <= i < GROUPS:
+                    normalise(i, range(0, 1))
+                if i + 1 < GROUPS:
+                    statistics(i + 1)
+                if 0 <= i < GROUPS:
+                    normalise(i, range(1, J))
+                if 0 <= i - 2:
+                    leave_psum(i - 2)
+                if 0 <= i - 1 < GROUPS:
+                    regroup(i - 1)
+                if 0 <= i - 2:
+                    gate_and_store(i - 2)
+                if 0 <= i < GROUPS:
+                    turn_and_scale(i)
+                if 0 <= i - 1 < GROUPS:
+                    quantise(i - 1, 0)
+                    quantise(i - 1, 1)

@@ -27,7 +27,7 @@ W = 2 * QK + 2 * E
 EPS = 1e-5
 BN_MAX = 512
 
-ROWS_VECTOR = 256
+HALF = GROUP // 2
 LOADS_AHEAD = 3
 
 FLOPS = 2 * ROWS * D * W
@@ -53,17 +53,19 @@ def tile_latentattentionblock_pa_t_kernel(tc, x, expand, ln_gamma, ln_beta, out_
 
         def load(s):
             x_sb = x_pool.tile([P, J, D], BF16)
-            nc.sync.dma_start(
-                out=x_sb[:], in_=x_rows[s * GROUP : (s + 1) * GROUP, :].rearrange("(p j) k -> p j k", j=J)
-            )
+            rows = x_rows[s * GROUP : (s + 1) * GROUP, :].rearrange("(p j) k -> p j k", j=J)
+            for j in range(J):
+                nc.sync.dma_start(out=x_sb[:, j, :], in_=rows[:, j, :])
             live["x", s] = x_sb
 
-        def partial_statistics(s):
-            stats = small.tile([P, J, D // BN_MAX, 6], F32)
-            for j in range(J):
+        def partial_statistics(s, row_tiles):
+            if ("stats", s) not in live:
+                live["stats", s] = small.tile([P, J, D // BN_MAX, 6], F32, name="stats")
+            for j in row_tiles:
                 for b in range(D // BN_MAX):
-                    nc.vector.bn_stats(out=stats[:, j, b, :], in_=live["x", s][:, j, b * BN_MAX : (b + 1) * BN_MAX])
-            live["stats", s] = stats
+                    nc.vector.bn_stats(
+                        out=live["stats", s][:, j, b, :], in_=live["x", s][:, j, b * BN_MAX : (b + 1) * BN_MAX]
+                    )
 
         def statistics(s):
             mean_var = small.tile([P, J, 2], F32)
@@ -76,18 +78,18 @@ def tile_latentattentionblock_pa_t_kernel(tc, x, expand, ln_gamma, ln_beta, out_
             live["mean_var", s] = mean_var
             live["rstd", s] = rstd
 
-        def normalise(s, row_tiles):
-            if ("z", s) not in live:
-                live["z", s] = z_pool.tile([P, J, D], F32, name="z")
-            for j in row_tiles:
+        def normalise(s):
+            z = z_pool.tile([P, J, D], F32)
+            for j in range(J):
                 nc.vector.tensor_scalar(
-                    out=live["z", s][:, j, :],
+                    out=z[:, j, :],
                     in0=live["x", s][:, j, :],
                     scalar1=live["mean_var", s][:, j, 0:1],
                     scalar2=live["rstd", s][:, j : j + 1],
                     op0=ALU.subtract,
                     op1=ALU.mult,
                 )
+            live["z", s] = z
 
         def turn_and_scale(s):
             z = live["z", s]
@@ -108,15 +110,27 @@ def tile_latentattentionblock_pa_t_kernel(tc, x, expand, ln_gamma, ln_beta, out_
         def regroup(s):
             h_turned = live["h_turned", s]
             h_grouped = h_pool.tile([P, PASSES, GROUP, PACK], BF16, align_bytes=64)
-            for copy, g, first, last in (
-                (nc.vector.tensor_copy, 0, 0, ROWS_VECTOR),
-                (nc.scalar.copy, 0, ROWS_VECTOR, GROUP),
-                (nc.scalar.copy, 1, 0, GROUP),
-            ):
-                copy(
-                    out=h_grouped[:, g, first:last, :].rearrange("p (r i) t -> p r t i", i=4),
-                    in_=h_turned[:, PACK * g : PACK * (g + 1), first:last].rearrange("p t (r i) -> p r t i", i=4),
-                )
+            for g in range(PASSES):
+                for half in range(2):
+                    rows = slice(half * HALF, (half + 1) * HALF)
+                    pieces = h_turned[:, PACK * g : PACK * (g + 1), rows]
+                    words = h_grouped[:, g, rows, :]
+                    if (g, half) == (0, 0):
+                        nc.gpsimd.tensor_scalar(
+                            out=words,
+                            in0=pieces.rearrange("p t r -> p r t"),
+                            scalar1=1.0,
+                            scalar2=0.0,
+                            op0=ALU.mult,
+                            op1=ALU.add,
+                        )
+                    else:
+                        scalars = (g, half) == (1, 1) or s < GROUPS - 2
+                        copy = nc.scalar.copy if scalars else nc.vector.tensor_copy
+                        copy(
+                            out=words.rearrange("p (r i) t -> p r t i", i=4),
+                            in_=pieces.rearrange("p t (r i) -> p r t i", i=4),
+                        )
             live["h_grouped", s] = h_grouped
             live["h_codes", s] = mx_pool.tile([P, PASSES, GROUP], U32, align_bytes=64, name="h_codes")
             live["h_scales", s] = mx_pool.tile([P, PASSES, GROUP], U8, align_bytes=64, name="h_scales")
@@ -224,21 +238,20 @@ def tile_latentattentionblock_pa_t_kernel(tc, x, expand, ln_gamma, ln_beta, out_
                 if i + 1 + LOADS_AHEAD < GROUPS:
                     load(i + 1 + LOADS_AHEAD)
                 if i + 1 < GROUPS:
-                    partial_statistics(i + 1)
+                    partial_statistics(i + 1, range(0, J // 2))
                 if 0 <= i - 2:
                     project(i - 2)
                 if 0 <= i < GROUPS:
-                    normalise(i, range(0, 1))
+                    normalise(i)
                 if i + 1 < GROUPS:
-                    statistics(i + 1)
-                if 0 <= i < GROUPS:
-                    normalise(i, range(1, J))
-                if 0 <= i - 2:
-                    leave_psum(i - 2)
+                    partial_statistics(i + 1, range(J // 2, J))
                 if 0 <= i - 1 < GROUPS:
                     regroup(i - 1)
                 if 0 <= i - 2:
+                    leave_psum(i - 2)
                     gate_and_store(i - 2)
+                if i + 1 < GROUPS:
+                    statistics(i + 1)
                 if 0 <= i < GROUPS:
                     turn_and_scale(i)
                 if 0 <= i - 1 < GROUPS:

@@ -17,9 +17,10 @@ ROWS = 8 * 1024
 D = 1024
 CHUNKS = D // P
 PASSES = CHUNKS // PACK
-J = 4
-GROUP = J * P
-GROUPS = ROWS // GROUP
+JMAX = 4
+TILES = [1, 1, 2, 2, 2] + [JMAX] * 13 + [2, 1, 1]
+GROUPS = len(TILES)
+FIRST = [sum(TILES[:s]) for s in range(GROUPS)]
 QK = 64
 E = 64
 V = 32
@@ -27,8 +28,7 @@ W = 2 * QK + 2 * E
 EPS = 1e-5
 BN_MAX = 512
 
-HALF = GROUP // 2
-LOADS_AHEAD = 3
+LOADS_AHEAD = 4
 
 FLOPS = 2 * ROWS * D * W
 
@@ -40,7 +40,7 @@ def tile_latentattentionblock_pa_t_kernel(tc, x, expand, ln_gamma, ln_beta, out_
 
     with ExitStack() as stack:
         const = stack.enter_context(tc.tile_pool(name="const", bufs=1))
-        x_pool = stack.enter_context(tc.tile_pool(name="x", bufs=4))
+        x_pool = stack.enter_context(tc.tile_pool(name="x", bufs=6))
         small = stack.enter_context(tc.tile_pool(name="small", bufs=3))
         z_pool = stack.enter_context(tc.tile_pool(name="z", bufs=2))
         h_pool = stack.enter_context(tc.tile_pool(name="h", bufs=2))
@@ -51,16 +51,23 @@ def tile_latentattentionblock_pa_t_kernel(tc, x, expand, ln_gamma, ln_beta, out_
 
         live = {}
 
+        def rows_of(s):
+            return slice(FIRST[s] * P, (FIRST[s] + TILES[s]) * P)
+
+        def first_half(s):
+            return (TILES[s] + 1) // 2
+
         def load(s):
+            J = TILES[s]
             x_sb = x_pool.tile([P, J, D], BF16)
-            rows = x_rows[s * GROUP : (s + 1) * GROUP, :].rearrange("(p j) k -> p j k", j=J)
+            rows = x_rows[rows_of(s), :].rearrange("(p j) k -> p j k", j=J)
             for j in range(J):
                 nc.sync.dma_start(out=x_sb[:, j, :], in_=rows[:, j, :])
             live["x", s] = x_sb
 
         def partial_statistics(s, row_tiles):
             if ("stats", s) not in live:
-                live["stats", s] = small.tile([P, J, D // BN_MAX, 6], F32, name="stats")
+                live["stats", s] = small.tile([P, TILES[s], D // BN_MAX, 6], F32, name="stats")
             for j in row_tiles:
                 for b in range(D // BN_MAX):
                     nc.vector.bn_stats(
@@ -68,17 +75,19 @@ def tile_latentattentionblock_pa_t_kernel(tc, x, expand, ln_gamma, ln_beta, out_
                     )
 
         def statistics(s):
+            J = TILES[s]
             mean_var = small.tile([P, J, 2], F32)
             for j in range(J):
                 nc.vector.bn_aggr(out=mean_var[:, j, :], in_=live["stats", s][:, j, :, :].rearrange("p b s -> p (b s)"))
             var_eps = small.tile([P, J], F32)
             nc.gpsimd.tensor_scalar(out=var_eps[:], in0=mean_var[:, :, 1], scalar1=EPS, scalar2=None, op0=ALU.add)
             rstd = small.tile([P, J], F32)
-            nc.gpsimd.tensor_tensor(out=rstd[:], in0=var_eps[:], in1=minus_half[:], op=ALU.pow)
+            nc.gpsimd.tensor_tensor(out=rstd[:], in0=var_eps[:], in1=minus_half[:, 0:J], op=ALU.pow)
             live["mean_var", s] = mean_var
             live["rstd", s] = rstd
 
         def normalise(s):
+            J = TILES[s]
             z = z_pool.tile([P, J, D], F32)
             for j in range(J):
                 nc.vector.tensor_scalar(
@@ -92,8 +101,9 @@ def tile_latentattentionblock_pa_t_kernel(tc, x, expand, ln_gamma, ln_beta, out_
             live["z", s] = z
 
         def turn_and_scale(s):
+            J = TILES[s]
             z = live["z", s]
-            h_turned = h_pool.tile([P, CHUNKS, GROUP], BF16)
+            h_turned = h_pool.tile([P, CHUNKS, J * P], BF16)
             for c in range(CHUNKS):
                 z_turned = turn.tile([P, J, P], F32, tag="bank")
                 for j in range(J):
@@ -108,14 +118,18 @@ def tile_latentattentionblock_pa_t_kernel(tc, x, expand, ln_gamma, ln_beta, out_
             live["h_turned", s] = h_turned
 
         def regroup(s):
+            rows_here = TILES[s] * P
+            half_rows = rows_here // 2
             h_turned = live["h_turned", s]
-            h_grouped = h_pool.tile([P, PASSES, GROUP, PACK], BF16, align_bytes=64)
+            h_grouped = h_pool.tile([P, PASSES, rows_here, PACK], BF16, align_bytes=64)
+            engines = "GSSS" if s < GROUPS - 4 else "GVVS" if s < GROUPS - 2 else "VVVS"
             for g in range(PASSES):
                 for half in range(2):
-                    rows = slice(half * HALF, (half + 1) * HALF)
+                    rows = slice(half * half_rows, (half + 1) * half_rows)
                     pieces = h_turned[:, PACK * g : PACK * (g + 1), rows]
                     words = h_grouped[:, g, rows, :]
-                    if (g, half) == (0, 0):
+                    engine = engines[2 * g + half]
+                    if engine == "G":
                         nc.gpsimd.tensor_scalar(
                             out=words,
                             in0=pieces.rearrange("p t r -> p r t"),
@@ -125,15 +139,14 @@ def tile_latentattentionblock_pa_t_kernel(tc, x, expand, ln_gamma, ln_beta, out_
                             op1=ALU.add,
                         )
                     else:
-                        scalars = (g, half) == (1, 1) or s < GROUPS - 2
-                        copy = nc.scalar.copy if scalars else nc.vector.tensor_copy
+                        copy = nc.scalar.copy if engine == "S" else nc.vector.tensor_copy
                         copy(
                             out=words.rearrange("p (r i) t -> p r t i", i=4),
                             in_=pieces.rearrange("p t (r i) -> p r t i", i=4),
                         )
             live["h_grouped", s] = h_grouped
-            live["h_codes", s] = mx_pool.tile([P, PASSES, GROUP], U32, align_bytes=64, name="h_codes")
-            live["h_scales", s] = mx_pool.tile([P, PASSES, GROUP], U8, align_bytes=64, name="h_scales")
+            live["h_codes", s] = mx_pool.tile([P, PASSES, rows_here], U32, align_bytes=64, name="h_codes")
+            live["h_scales", s] = mx_pool.tile([P, PASSES, rows_here], U8, align_bytes=64, name="h_scales")
 
         def quantise(s, g):
             nc.vector.quantize_mx(
@@ -143,6 +156,7 @@ def tile_latentattentionblock_pa_t_kernel(tc, x, expand, ln_gamma, ln_beta, out_
             )
 
         def project(s):
+            J = TILES[s]
             h_codes, h_scales = live["h_codes", s], live["h_scales", s]
             proj_qk = acc.tile([P, J, 2 * QK], F32)
             proj_gate = acc.tile([P, J, 2 * E], F32)
@@ -162,6 +176,7 @@ def tile_latentattentionblock_pa_t_kernel(tc, x, expand, ln_gamma, ln_beta, out_
             live["proj_gate", s] = proj_gate
 
         def leave_psum(s):
+            J = TILES[s]
             proj_qk = live["proj_qk", s]
             qk_sb = out_pool.tile([P, 2, J, QK], F32)
             nc.scalar.copy(
@@ -174,6 +189,7 @@ def tile_latentattentionblock_pa_t_kernel(tc, x, expand, ln_gamma, ln_beta, out_
             live["gelu_sb", s] = gelu_sb
 
         def gate_and_store(s):
+            J = TILES[s]
             proj_gate, gelu_sb, qk_sb = live["proj_gate", s], live["gelu_sb", s], live["qk_sb", s]
             geglu_sb = out_pool.tile([P, 2, J, V], F32)
             nc.vector.tensor_tensor(
@@ -182,7 +198,7 @@ def tile_latentattentionblock_pa_t_kernel(tc, x, expand, ln_gamma, ln_beta, out_
                 in1=gelu_sb[:].rearrange("p j (v c) -> p j v c", v=2),
                 op=ALU.mult,
             )
-            rows = slice(s * GROUP, (s + 1) * GROUP)
+            rows = rows_of(s)
             for plane in range(2):
                 nc.sync.dma_start(
                     out=outs[plane][rows, :].rearrange("(p j) c -> p (j c)", j=J),
@@ -196,24 +212,27 @@ def tile_latentattentionblock_pa_t_kernel(tc, x, expand, ln_gamma, ln_beta, out_
         for s in range(LOADS_AHEAD):
             load(s)
 
+        e_sb = const.tile([P, W // P, D], BF16)
+        nc.scalar.dma_start(out=e_sb[:], in_=expand.rearrange("(h f) k -> f h k", f=P))
         ident_f32 = const.tile([P, P], F32)
         make_identity(nc, ident_f32[:])
         ident_bf16 = const.tile([P, P], BF16)
         make_identity(nc, ident_bf16[:])
-        minus_half = const.tile([P, J], F32)
+        minus_half = const.tile([P, JMAX], F32)
         nc.vector.memset(minus_half[:], -0.5)
 
         vec_rows = const.tile([P, P], BF16)
         nc.vector.memset(vec_rows[:], 0.0)
         nc.scalar.dma_start(out=vec_rows[0:CHUNKS, :], in_=ln_gamma.rearrange("(c p) -> c p", p=P))
         nc.scalar.dma_start(out=vec_rows[CHUNKS : 2 * CHUNKS, :], in_=ln_beta.rearrange("(c p) -> c p", p=P))
+        table = const.tile([P, 1], F32)
+        nc.scalar.activation(out=table[:], in_=minus_half[:, 0:1], func=ACT.Gelu)
+
         vec_cols = turn.tile([P, P], BF16, tag="bank")
         nc.tensor.transpose(vec_cols[:], vec_rows[:], ident_bf16[:])
         gain_shift = const.tile([P, 2 * CHUNKS], F32)
-        nc.vector.tensor_copy(out=gain_shift[:], in_=vec_cols[:, 0 : 2 * CHUNKS])
+        nc.scalar.copy(out=gain_shift[:], in_=vec_cols[:, 0 : 2 * CHUNKS])
 
-        e_sb = const.tile([P, W // P, D], BF16)
-        nc.scalar.dma_start(out=e_sb[:], in_=expand.rearrange("(h f) k -> f h k", f=P))
         e_grouped = const.tile([P, PASSES, W, PACK], BF16, align_bytes=64)
         for g in range(PASSES):
             for half in range(W // P):
@@ -221,30 +240,34 @@ def tile_latentattentionblock_pa_t_kernel(tc, x, expand, ln_gamma, ln_beta, out_
                 for t in range(PACK):
                     c = PACK * g + t
                     nc.tensor.transpose(e_turned[:, t, :], e_sb[:, half, c * P : (c + 1) * P], ident_bf16[:])
-                nc.vector.tensor_copy(
+                nc.scalar.copy(
                     out=e_grouped[:, g, half * P : (half + 1) * P, :],
                     in_=e_turned[:].rearrange("p t f -> p f t"),
                 )
         e_codes = const.tile([P, PASSES, W], U32, align_bytes=64)
         e_scales = const.tile([P, PASSES, W], U8, align_bytes=64)
-        nc.vector.quantize_mx(
-            out=e_codes[:].rearrange("p g f -> p (g f)").bitcast(FP8X4),
-            scales=e_scales[:].rearrange("p g f -> p (g f)"),
-            in_=e_grouped[:].rearrange("p g f t -> p (g f t)"),
-        )
+
+        def quantise_expand():
+            nc.vector.quantize_mx(
+                out=e_codes[:].rearrange("p g f -> p (g f)").bitcast(FP8X4),
+                scales=e_scales[:].rearrange("p g f -> p (g f)"),
+                in_=e_grouped[:].rearrange("p g f t -> p (g f t)"),
+            )
 
         with tc.manual_schedule():
             for i in range(-1, GROUPS + 2):
                 if i + 1 + LOADS_AHEAD < GROUPS:
                     load(i + 1 + LOADS_AHEAD)
                 if i + 1 < GROUPS:
-                    partial_statistics(i + 1, range(0, J // 2))
+                    partial_statistics(i + 1, range(0, first_half(i + 1)))
+                if i == 2:
+                    quantise_expand()
                 if 0 <= i - 2:
                     project(i - 2)
                 if 0 <= i < GROUPS:
                     normalise(i)
                 if i + 1 < GROUPS:
-                    partial_statistics(i + 1, range(J // 2, J))
+                    partial_statistics(i + 1, range(first_half(i + 1), TILES[i + 1]))
                 if 0 <= i - 1 < GROUPS:
                     regroup(i - 1)
                 if 0 <= i - 2:

@@ -18,7 +18,7 @@ D = 1024
 CHUNKS = D // P
 PASSES = CHUNKS // PACK
 JMAX = 4
-TILES = [1, 1, 2, 2, 2] + [JMAX] * 13 + [2, 1, 1]
+TILES = [2, 2, 2, 2] + [JMAX] * 13 + [2, 1, 1]
 GROUPS = len(TILES)
 FIRST = [sum(TILES[:s]) for s in range(GROUPS)]
 QK = 64
@@ -28,6 +28,7 @@ W = 2 * QK + 2 * E
 EPS = 1e-5
 BN_MAX = 512
 
+VECTOR_REGROUPS = 5
 LOADS_AHEAD = 4
 
 FLOPS = 2 * ROWS * D * W
@@ -119,40 +120,41 @@ def tile_latentattentionblock_pa_t_kernel(tc, x, expand, ln_gamma, ln_beta, out_
 
         def regroup(s):
             rows_here = TILES[s] * P
-            half_rows = rows_here // 2
+            lower, upper, every = slice(0, rows_here // 2), slice(rows_here // 2, rows_here), slice(0, rows_here)
+            if s < GROUPS - VECTOR_REGROUPS:
+                shares = ((nc.gpsimd, 0, lower), (nc.scalar, 0, upper), (nc.scalar, 1, every))
+            else:
+                shares = ((nc.vector, 0, every), (nc.vector, 1, lower), (nc.scalar, 1, upper))
             h_turned = live["h_turned", s]
             h_grouped = h_pool.tile([P, PASSES, rows_here, PACK], BF16, align_bytes=64)
-            engines = "GSSS" if s < GROUPS - 4 else "GVVS" if s < GROUPS - 2 else "VVVS"
-            for g in range(PASSES):
-                for half in range(2):
-                    rows = slice(half * half_rows, (half + 1) * half_rows)
-                    pieces = h_turned[:, PACK * g : PACK * (g + 1), rows]
-                    words = h_grouped[:, g, rows, :]
-                    engine = engines[2 * g + half]
-                    if engine == "G":
-                        nc.gpsimd.tensor_scalar(
-                            out=words,
-                            in0=pieces.rearrange("p t r -> p r t"),
-                            scalar1=1.0,
-                            scalar2=0.0,
-                            op0=ALU.mult,
-                            op1=ALU.add,
-                        )
-                    else:
-                        copy = nc.scalar.copy if engine == "S" else nc.vector.tensor_copy
-                        copy(
-                            out=words.rearrange("p (r i) t -> p r t i", i=4),
-                            in_=pieces.rearrange("p t (r i) -> p r t i", i=4),
-                        )
+            for engine, g, rows in shares:
+                pieces = h_turned[:, PACK * g : PACK * (g + 1), rows]
+                words = h_grouped[:, g, rows, :]
+                if engine is nc.scalar:
+                    nc.scalar.copy(
+                        out=words.rearrange("p (r i) t -> p r t i", i=4),
+                        in_=pieces.rearrange("p t (r i) -> p r t i", i=4),
+                    )
+                elif engine is nc.vector:
+                    nc.vector.tensor_copy(out=words, in_=pieces.rearrange("p t r -> p r t"))
+                else:
+                    nc.gpsimd.tensor_scalar(
+                        out=words,
+                        in0=pieces.rearrange("p t r -> p r t"),
+                        scalar1=1.0,
+                        scalar2=0.0,
+                        op0=ALU.mult,
+                        op1=ALU.add,
+                    )
             live["h_grouped", s] = h_grouped
             live["h_codes", s] = mx_pool.tile([P, PASSES, rows_here], U32, align_bytes=64, name="h_codes")
             live["h_scales", s] = mx_pool.tile([P, PASSES, rows_here], U8, align_bytes=64, name="h_scales")
 
-        def quantise(s, g):
+        def quantise(s):
             nc.vector.quantize_mx(
-                out=live["h_codes", s][:, g, :].bitcast(FP8X4),
-                scales=live["h_scales", s][:, g, :],
-                in_=live["h_grouped", s][:, g, :, :].rearrange("p r t -> p (r t)"),
+                out=live["h_codes", s][:].rearrange("p g r -> p (g r)").bitcast(FP8X4),
+                scales=live["h_scales", s][:].rearrange("p g r -> p (g r)"),
+                in_=live["h_grouped", s][:].rearrange("p g r t -> p (g r t)"),
             )
 
         def project(s):
@@ -278,5 +280,4 @@ def tile_latentattentionblock_pa_t_kernel(tc, x, expand, ln_gamma, ln_beta, out_
                 if 0 <= i < GROUPS:
                     turn_and_scale(i)
                 if 0 <= i - 1 < GROUPS:
-                    quantise(i - 1, 0)
-                    quantise(i - 1, 1)
+                    quantise(i - 1)

@@ -18,7 +18,7 @@ D = 1024
 CHUNKS = D // P
 PASSES = CHUNKS // PACK
 JMAX = 4
-TILES = [2, 2, 2, 2] + [JMAX] * 13 + [2, 1, 1]
+TILES = [2, 2] + [JMAX] * 14 + [2, 1, 1]
 GROUPS = len(TILES)
 FIRST = [sum(TILES[:s]) for s in range(GROUPS)]
 QK = 64
@@ -28,7 +28,7 @@ W = 2 * QK + 2 * E
 EPS = 1e-5
 BN_MAX = 512
 
-VECTOR_REGROUPS = 5
+VECTOR_REGROUPS = 4
 LOADS_AHEAD = 4
 
 FLOPS = 2 * ROWS * D * W
@@ -56,7 +56,7 @@ def tile_latentattentionblock_pa_t_kernel(tc, x, expand, ln_gamma, ln_beta, out_
             return slice(FIRST[s] * P, (FIRST[s] + TILES[s]) * P)
 
         def first_half(s):
-            return (TILES[s] + 1) // 2
+            return TILES[s] if s <= 1 else (TILES[s] + 1) // 2
 
         def load(s):
             J = TILES[s]
@@ -272,11 +272,11 @@ def tile_latentattentionblock_pa_t_kernel(tc, x, expand, ln_gamma, ln_beta, out_
                     partial_statistics(i + 1, range(first_half(i + 1), TILES[i + 1]))
                 if 0 <= i - 1 < GROUPS:
                     regroup(i - 1)
+                if i + 1 < GROUPS:
+                    statistics(i + 1)
                 if 0 <= i - 2:
                     leave_psum(i - 2)
                     gate_and_store(i - 2)
-                if i + 1 < GROUPS:
-                    statistics(i + 1)
                 if 0 <= i < GROUPS:
                     turn_and_scale(i)
                 if 0 <= i - 1 < GROUPS:

from contextlib import ExitStack

import concourse.mybir as mybir
from concourse.masks import make_identity

F32 = mybir.dt.float32
BF16 = mybir.dt.bfloat16
U32 = mybir.dt.uint32
U8 = mybir.dt.uint8
FP8X4 = mybir.dt.float8_e4m3fn_x4
ALU = mybir.AluOpType
ACT = mybir.ActivationFunctionType

P = 128
PACK = 4
ROWS = 8 * 1024
D = 1024
CHUNKS = D // P
PASSES = CHUNKS // PACK
JMAX = 4
TILES = [2, 2] + [JMAX] * 14 + [2, 1, 1]
GROUPS = len(TILES)
FIRST = [sum(TILES[:s]) for s in range(GROUPS)]
QK = 64
E = 64
V = 32
W = 2 * QK + 2 * E
EPS = 1e-5
BN_MAX = 512

VECTOR_REGROUPS = 4
LOADS_AHEAD = 4

FLOPS = 2 * ROWS * D * W


def tile_latentattentionblock_pa_t_kernel(tc, x, expand, ln_gamma, ln_beta, out_0, out_1, out_2, out_3):
    nc = tc.nc
    x_rows = x.flatten_outer_dims()
    outs = [o.flatten_outer_dims() for o in (out_0, out_1, out_2, out_3)]

    with ExitStack() as stack:
        const = stack.enter_context(tc.tile_pool(name="const", bufs=1))
        x_pool = stack.enter_context(tc.tile_pool(name="x", bufs=6))
        small = stack.enter_context(tc.tile_pool(name="small", bufs=3))
        z_pool = stack.enter_context(tc.tile_pool(name="z", bufs=2))
        h_pool = stack.enter_context(tc.tile_pool(name="h", bufs=2))
        mx_pool = stack.enter_context(tc.tile_pool(name="mx", bufs=2))
        out_pool = stack.enter_context(tc.tile_pool(name="out", bufs=3))
        turn = stack.enter_context(tc.psum_pool(name="turn", bufs=6))
        acc = stack.enter_context(tc.psum_pool(name="acc", bufs=1))

        live = {}

        def rows_of(s):
            return slice(FIRST[s] * P, (FIRST[s] + TILES[s]) * P)

        def first_half(s):
            return TILES[s] if s <= 1 else (TILES[s] + 1) // 2

        def load(s):
            J = TILES[s]
            x_sb = x_pool.tile([P, J, D], BF16)
            rows = x_rows[rows_of(s), :].rearrange("(p j) k -> p j k", j=J)
            for j in range(J):
                nc.sync.dma_start(out=x_sb[:, j, :], in_=rows[:, j, :])
            live["x", s] = x_sb

        def partial_statistics(s, row_tiles):
            if ("stats", s) not in live:
                live["stats", s] = small.tile([P, TILES[s], D // BN_MAX, 6], F32, name="stats")
            for j in row_tiles:
                for b in range(D // BN_MAX):
                    nc.vector.bn_stats(
                        out=live["stats", s][:, j, b, :], in_=live["x", s][:, j, b * BN_MAX : (b + 1) * BN_MAX]
                    )

        def statistics(s):
            J = TILES[s]
            mean_var = small.tile([P, J, 2], F32)
            for j in range(J):
                nc.vector.bn_aggr(out=mean_var[:, j, :], in_=live["stats", s][:, j, :, :].rearrange("p b s -> p (b s)"))
            var_eps = small.tile([P, J], F32)
            nc.gpsimd.tensor_scalar(out=var_eps[:], in0=mean_var[:, :, 1], scalar1=EPS, scalar2=None, op0=ALU.add)
            rstd = small.tile([P, J], F32)
            nc.gpsimd.tensor_tensor(out=rstd[:], in0=var_eps[:], in1=minus_half[:, 0:J], op=ALU.pow)
            live["mean_var", s] = mean_var
            live["rstd", s] = rstd

        def normalise(s):
            J = TILES[s]
            z = z_pool.tile([P, J, D], F32)
            for j in range(J):
                nc.vector.tensor_scalar(
                    out=z[:, j, :],
                    in0=live["x", s][:, j, :],
                    scalar1=live["mean_var", s][:, j, 0:1],
                    scalar2=live["rstd", s][:, j : j + 1],
                    op0=ALU.subtract,
                    op1=ALU.mult,
                )
            live["z", s] = z

        def turn_and_scale(s):
            J = TILES[s]
            z = live["z", s]
            h_turned = h_pool.tile([P, CHUNKS, J * P], BF16)
            for c in range(CHUNKS):
                z_turned = turn.tile([P, J, P], F32, tag="bank")
                for j in range(J):
                    nc.tensor.transpose(z_turned[:, j, :], z[:, j, c * P : (c + 1) * P], ident_f32[:])
                nc.scalar.activation(
                    out=h_turned[:, c, :],
                    in_=z_turned[:].rearrange("p j r -> p (j r)"),
                    func=ACT.Identity,
                    bias=gain_shift[:, CHUNKS + c : CHUNKS + c + 1],
                    scale=gain_shift[:, c : c + 1],
                )
            live["h_turned", s] = h_turned

        def regroup(s):
            rows_here = TILES[s] * P
            lower, upper, every = slice(0, rows_here // 2), slice(rows_here // 2, rows_here), slice(0, rows_here)
            if s < GROUPS - VECTOR_REGROUPS:
                shares = ((nc.gpsimd, 0, lower), (nc.scalar, 0, upper), (nc.scalar, 1, every))
            else:
                shares = ((nc.vector, 0, every), (nc.vector, 1, lower), (nc.scalar, 1, upper))
            h_turned = live["h_turned", s]
            h_grouped = h_pool.tile([P, PASSES, rows_here, PACK], BF16, align_bytes=64)
            for engine, g, rows in shares:
                pieces = h_turned[:, PACK * g : PACK * (g + 1), rows]
                words = h_grouped[:, g, rows, :]
                if engine is nc.scalar:
                    nc.scalar.copy(
                        out=words.rearrange("p (r i) t -> p r t i", i=4),
                        in_=pieces.rearrange("p t (r i) -> p r t i", i=4),
                    )
                elif engine is nc.vector:
                    nc.vector.tensor_copy(out=words, in_=pieces.rearrange("p t r -> p r t"))
                else:
                    nc.gpsimd.tensor_scalar(
                        out=words,
                        in0=pieces.rearrange("p t r -> p r t"),
                        scalar1=1.0,
                        scalar2=0.0,
                        op0=ALU.mult,
                        op1=ALU.add,
                    )
            live["h_grouped", s] = h_grouped
            live["h_codes", s] = mx_pool.tile([P, PASSES, rows_here], U32, align_bytes=64, name="h_codes")
            live["h_scales", s] = mx_pool.tile([P, PASSES, rows_here], U8, align_bytes=64, name="h_scales")

        def quantise(s):
            nc.vector.quantize_mx(
                out=live["h_codes", s][:].rearrange("p g r -> p (g r)").bitcast(FP8X4),
                scales=live["h_scales", s][:].rearrange("p g r -> p (g r)"),
                in_=live["h_grouped", s][:].rearrange("p g r t -> p (g r t)"),
            )

        def project(s):
            J = TILES[s]
            h_codes, h_scales = live["h_codes", s], live["h_scales", s]
            proj_qk = acc.tile([P, J, 2 * QK], F32)
            proj_gate = acc.tile([P, J, 2 * E], F32)
            for j in range(J):
                for bank, first in ((proj_qk, 0), (proj_gate, 2 * QK)):
                    for g in range(PASSES):
                        nc.tensor.matmul_mx(
                            out=bank[:, j, :],
                            lhsT=h_codes[:, g, j * P : (j + 1) * P].bitcast(FP8X4),
                            lhsT_scale=h_scales[:, g, j * P : (j + 1) * P],
                            rhs=e_codes[:, g, first : first + P].bitcast(FP8X4),
                            rhs_scale=e_scales[:, g, first : first + P],
                            start=(g == 0),
                            stop=(g == PASSES - 1),
                        )
            live["proj_qk", s] = proj_qk
            live["proj_gate", s] = proj_gate

        def leave_psum(s):
            J = TILES[s]
            proj_qk = live["proj_qk", s]
            qk_sb = out_pool.tile([P, 2, J, QK], F32)
            nc.scalar.copy(
                out=qk_sb[:].rearrange("p w j c -> p j w c"),
                in_=proj_qk[:].rearrange("p j (w c) -> p j w c", w=2),
            )
            gelu_sb = out_pool.tile([P, J, E], F32)
            nc.scalar.activation(out=gelu_sb[:], in_=live["proj_gate", s][:, :, E : 2 * E], func=ACT.Gelu)
            live["qk_sb", s] = qk_sb
            live["gelu_sb", s] = gelu_sb

        def gate_and_store(s):
            J = TILES[s]
            proj_gate, gelu_sb, qk_sb = live["proj_gate", s], live["gelu_sb", s], live["qk_sb", s]
            geglu_sb = out_pool.tile([P, 2, J, V], F32)
            nc.vector.tensor_tensor(
                out=geglu_sb[:].rearrange("p v j c -> p j v c"),
                in0=proj_gate[:, :, 0:E].rearrange("p j (v c) -> p j v c", v=2),
                in1=gelu_sb[:].rearrange("p j (v c) -> p j v c", v=2),
                op=ALU.mult,
            )
            rows = rows_of(s)
            for plane in range(2):
                nc.sync.dma_start(
                    out=outs[plane][rows, :].rearrange("(p j) c -> p (j c)", j=J),
                    in_=qk_sb[:, plane, :, :].rearrange("p j c -> p (j c)"),
                )
                nc.sync.dma_start(
                    out=outs[2 + plane][rows, :].rearrange("(p j) c -> p (j c)", j=J),
                    in_=geglu_sb[:, plane, :, :].rearrange("p j c -> p (j c)"),
                )

        for s in range(LOADS_AHEAD):
            load(s)

        e_sb = const.tile([P, W // P, D], BF16)
        nc.scalar.dma_start(out=e_sb[:], in_=expand.rearrange("(h f) k -> f h k", f=P))
        ident_f32 = const.tile([P, P], F32)
        make_identity(nc, ident_f32[:])
        ident_bf16 = const.tile([P, P], BF16)
        make_identity(nc, ident_bf16[:])
        minus_half = const.tile([P, JMAX], F32)
        nc.vector.memset(minus_half[:], -0.5)

        vec_rows = const.tile([P, P], BF16)
        nc.vector.memset(vec_rows[:], 0.0)
        nc.scalar.dma_start(out=vec_rows[0:CHUNKS, :], in_=ln_gamma.rearrange("(c p) -> c p", p=P))
        nc.scalar.dma_start(out=vec_rows[CHUNKS : 2 * CHUNKS, :], in_=ln_beta.rearrange("(c p) -> c p", p=P))
        table = const.tile([P, 1], F32)
        nc.scalar.activation(out=table[:], in_=minus_half[:, 0:1], func=ACT.Gelu)

        vec_cols = turn.tile([P, P], BF16, tag="bank")
        nc.tensor.transpose(vec_cols[:], vec_rows[:], ident_bf16[:])
        gain_shift = const.tile([P, 2 * CHUNKS], F32)
        nc.scalar.copy(out=gain_shift[:], in_=vec_cols[:, 0 : 2 * CHUNKS])

        e_grouped = const.tile([P, PASSES, W, PACK], BF16, align_bytes=64)
        for g in range(PASSES):
            for half in range(W // P):
                e_turned = turn.tile([P, PACK, P], BF16, tag="bank")
                for t in range(PACK):
                    c = PACK * g + t
                    nc.tensor.transpose(e_turned[:, t, :], e_sb[:, half, c * P : (c + 1) * P], ident_bf16[:])
                nc.scalar.copy(
                    out=e_grouped[:, g, half * P : (half + 1) * P, :],
                    in_=e_turned[:].rearrange("p t f -> p f t"),
                )
        e_codes = const.tile([P, PASSES, W], U32, align_bytes=64)
        e_scales = const.tile([P, PASSES, W], U8, align_bytes=64)

        def quantise_expand():
            nc.vector.quantize_mx(
                out=e_codes[:].rearrange("p g f -> p (g f)").bitcast(FP8X4),
                scales=e_scales[:].rearrange("p g f -> p (g f)"),
                in_=e_grouped[:].rearrange("p g f t -> p (g f t)"),
            )

        with tc.manual_schedule():
            for i in range(-1, GROUPS + 2):
                if i + 1 + LOADS_AHEAD < GROUPS:
                    load(i + 1 + LOADS_AHEAD)
                if i + 1 < GROUPS:
                    partial_statistics(i + 1, range(0, first_half(i + 1)))
                if i == 2:
                    quantise_expand()
                if 0 <= i - 2:
                    project(i - 2)
                if 0 <= i < GROUPS:
                    normalise(i)
                if i + 1 < GROUPS:
                    partial_statistics(i + 1, range(first_half(i + 1), TILES[i + 1]))
                if 0 <= i - 1 < GROUPS:
                    regroup(i - 1)
                if i + 1 < GROUPS:
                    statistics(i + 1)
                if 0 <= i - 2:
                    leave_psum(i - 2)
                    gate_and_store(i - 2)
                if 0 <= i < GROUPS:
                    turn_and_scale(i)
                if 0 <= i - 1 < GROUPS:
                    quantise(i - 1)
